import numpy as np
import ml_dtypes

BF16 = ml_dtypes.bfloat16


def bf(x):
    return np.asarray(x, np.float32).astype(BF16)


def f32(x):
    return np.asarray(x, np.float32)


def f64(x):
    return np.asarray(x).astype(np.float64)


def striped(idx):
    return np.tile(idx.reshape(-1, 16).T, (8, 1))


C, S, N, T = 128, 4096, 2048, 5
GAMMA = 0.99


def setup_inputs():
    return {"next_q": f32(np.random.standard_normal((C, S))), "reward": f32(np.random.standard_normal((T, N))), "done": f32(0.8 * np.random.random((1, N))), "offs": striped(np.random.permutation(np.tile(np.arange(S), 2))[:N])}


def reference(next_q, reward, done, offs):
    idx = offs[:16].T.reshape(-1)
    factor = GAMMA ** np.arange(T, dtype=np.float64)
    r = factor[None, :] @ f64(reward)
    coef = GAMMA ** T * (1.0 - f64(done))
    return f64(next_q)[:, idx] * coef + r

@@ -1,0 +1,60 @@
+import concourse.mybir as mybir
+
+F32 = mybir.dt.float32
+U16 = mybir.dt.uint16
+ALU = mybir.AluOpType
+
+QUANTILES = 128
+PAIRS = 4096
+SAMPLES = 2048
+STEPS = 5
+GAMMA = 0.99
+
+PIECE = 512
+PIECES = SAMPLES // PIECE
+OFFSETS_PER_COLUMN = 16
+
+
+def tile_qrdqnnsteptderror_kernel(tc, next_q, reward, done, offs, out):
+    nc = tc.nc
+    with (
+        tc.tile_pool(name="held", bufs=1) as held,
+        tc.tile_pool(name="moving", bufs=PIECES) as moving,
+        tc.psum_pool(name="psum", bufs=1) as psum,
+    ):
+        offsets = held.tile([QUANTILES, SAMPLES // OFFSETS_PER_COLUMN], U16, name="offsets")
+        nc.sync.dma_start(offsets[:], offs)
+        rewards = held.tile([STEPS, SAMPLES], F32, name="rewards")
+        nc.scalar.dma_start(rewards[:], reward)
+        done_all = held.tile([QUANTILES, SAMPLES], F32, name="done_all")
+        nc.sync.dma_start(done_all[:], done.squeeze(0).partition_broadcast(QUANTILES))
+        table = held.tile([QUANTILES, PAIRS], F32, name="table")
+        half = PAIRS // 2
+        nc.scalar.dma_start(table[:, :half], next_q[:, :half])
+        nc.sync.dma_start(table[:, half:], next_q[:, half:])
+
+        discount = held.tile([STEPS, QUANTILES], F32, name="discount")
+        for t in reversed(range(STEPS)):
+            nc.gpsimd.memset(discount[: t + 1, :], GAMMA**t)
+
+        r_all = [psum.tile([QUANTILES, PIECE], F32, name=f"r_all{i}") for i in range(PIECES)]
+        for i in range(PIECES):
+            columns = slice(i * PIECE, (i + 1) * PIECE)
+            nc.tensor.matmul(r_all[i][:], discount[:], rewards[:, columns], start=True, stop=True)
+
+        coef_all = held.tile([QUANTILES, SAMPLES], F32, name="coef_all")
+        nc.vector.tensor_scalar(
+            coef_all[:], done_all[:], 1.0, -(GAMMA**STEPS), ALU.subtract, ALU.mult
+        )
+
+        for i in range(PIECES):
+            columns = slice(i * PIECE, (i + 1) * PIECE)
+            entries = slice(i * PIECE // OFFSETS_PER_COLUMN, (i + 1) * PIECE // OFFSETS_PER_COLUMN)
+            damped = moving.tile([QUANTILES, PIECE], F32, name="damped")
+            nc.vector.tensor_tensor(
+                damped[:], table[:].indirect(offsets[:, entries]), coef_all[:, columns], ALU.mult
+            )
+            target = moving.tile([QUANTILES, PIECE], F32, name="target")
+            nc.vector.tensor_tensor(target[:], damped[:], r_all[i][:], ALU.add)
+            store_queue = nc.sync if i % 2 == 0 else nc.scalar
+            store_queue.dma_start(out[:, columns], target[:])

@@ -3,6 +3,7 @@ import concourse.mybir as mybir
 F32 = mybir.dt.float32
 U16 = mybir.dt.uint16
 ALU = mybir.AluOpType
+COPY = mybir.ActivationFunctionType.Copy
 
 QUANTILES = 128
 PAIRS = 4096
@@ -13,6 +14,7 @@ GAMMA = 0.99
 PIECE = 512
 PIECES = SAMPLES // PIECE
 OFFSETS_PER_COLUMN = 16
+ROWS = 128
 
 
 def tile_qrdqnnsteptderror_kernel(tc, next_q, reward, done, offs, out):
@@ -22,30 +24,45 @@ def tile_qrdqnnsteptderror_kernel(tc, next_q, reward, done, offs, out):
         tc.tile_pool(name="moving", bufs=PIECES) as moving,
         tc.psum_pool(name="psum", bufs=1) as psum,
     ):
+        loaded = held.tile([STEPS + 1, SAMPLES], F32, name="loaded")
+        nc.sync.dma_start(loaded[STEPS:, :], done)
+        nc.sync.dma_start(loaded[: STEPS - 1, :], reward[: STEPS - 1, :])
+        nc.sync.dma_start(loaded[STEPS - 1 : STEPS, :], reward[STEPS - 1 :, :])
         offsets = held.tile([QUANTILES, SAMPLES // OFFSETS_PER_COLUMN], U16, name="offsets")
         nc.sync.dma_start(offsets[:], offs)
-        rewards = held.tile([STEPS, SAMPLES], F32, name="rewards")
-        nc.scalar.dma_start(rewards[:], reward)
-        done_all = held.tile([QUANTILES, SAMPLES], F32, name="done_all")
-        nc.sync.dma_start(done_all[:], done.squeeze(0).partition_broadcast(QUANTILES))
         table = held.tile([QUANTILES, PAIRS], F32, name="table")
         half = PAIRS // 2
-        nc.scalar.dma_start(table[:, :half], next_q[:, :half])
+        nc.sync.dma_start(table[:, :half], next_q[:, :half])
         nc.sync.dma_start(table[:, half:], next_q[:, half:])
 
-        discount = held.tile([STEPS, QUANTILES], F32, name="discount")
+        stacked = held.tile([ROWS, SAMPLES], F32, name="stacked")
+        nc.vector.memset(stacked[:], 0.0)
+        for i in range(PIECES):
+            columns = slice(i * PIECE, (i + 1) * PIECE)
+            nc.vector.tensor_copy(stacked[: STEPS + 1, columns], loaded[:, columns])
+
+        pick_done = held.tile([ROWS, QUANTILES], F32, name="pick_done")
+        nc.gpsimd.memset(pick_done[:], 0.0)
+        nc.gpsimd.memset(pick_done[: STEPS + 1, :], 1.0)
+        nc.gpsimd.memset(pick_done[:STEPS, :], 0.0)
+        discount = held.tile([ROWS, QUANTILES], F32, name="discount")
+        nc.gpsimd.memset(discount[:], 0.0)
         for t in reversed(range(STEPS)):
             nc.gpsimd.memset(discount[: t + 1, :], GAMMA**t)
+
+        coef_all = held.tile([QUANTILES, SAMPLES], F32, name="coef_all")
+        for i in range(PIECES):
+            columns = slice(i * PIECE, (i + 1) * PIECE)
+            done_all = psum.tile([QUANTILES, PIECE], F32, name=f"done_all{i}")
+            nc.tensor.matmul(done_all[:], pick_done[:], stacked[:, columns], start=True, stop=True)
+            nc.scalar.activation(
+                coef_all[:, columns], done_all[:], COPY, bias=GAMMA**STEPS, scale=-(GAMMA**STEPS)
+            )
 
         r_all = [psum.tile([QUANTILES, PIECE], F32, name=f"r_all{i}") for i in range(PIECES)]
         for i in range(PIECES):
             columns = slice(i * PIECE, (i + 1) * PIECE)
-            nc.tensor.matmul(r_all[i][:], discount[:], rewards[:, columns], start=True, stop=True)
-
-        coef_all = held.tile([QUANTILES, SAMPLES], F32, name="coef_all")
-        nc.vector.tensor_scalar(
-            coef_all[:], done_all[:], 1.0, -(GAMMA**STEPS), ALU.subtract, ALU.mult
-        )
+            nc.tensor.matmul(r_all[i][:], discount[:], stacked[:, columns], start=True, stop=True)
 
         for i in range(PIECES):
             columns = slice(i * PIECE, (i + 1) * PIECE)

@@ -16,18 +16,20 @@ PIECES = SAMPLES // PIECE
 OFFSETS_PER_COLUMN = 16
 ROWS = 128
 
+WARMING_MATMULS = 3
+
+GPSIMD_PIECES = PIECES // 2
+
 
 def tile_qrdqnnsteptderror_kernel(tc, next_q, reward, done, offs, out):
     nc = tc.nc
     with (
         tc.tile_pool(name="held", bufs=1) as held,
-        tc.tile_pool(name="moving", bufs=PIECES) as moving,
-        tc.psum_pool(name="psum", bufs=1) as psum,
+        tc.psum_pool(name="psum_held", bufs=1) as psum_held,
+        tc.psum_pool(name="psum_moving", bufs=3) as psum_moving,
     ):
-        loaded = held.tile([STEPS + 1, SAMPLES], F32, name="loaded")
-        nc.sync.dma_start(loaded[STEPS:, :], done)
-        nc.sync.dma_start(loaded[: STEPS - 1, :], reward[: STEPS - 1, :])
-        nc.sync.dma_start(loaded[STEPS - 1 : STEPS, :], reward[STEPS - 1 :, :])
+        done_row = held.tile([1, SAMPLES], F32, name="done_row")
+        nc.sync.dma_start(done_row[:], done)
         offsets = held.tile([QUANTILES, SAMPLES // OFFSETS_PER_COLUMN], U16, name="offsets")
         nc.sync.dma_start(offsets[:], offs)
         table = held.tile([QUANTILES, PAIRS], F32, name="table")
@@ -35,43 +37,56 @@ def tile_qrdqnnsteptderror_kernel(tc, next_q, reward, done, offs, out):
         nc.sync.dma_start(table[:, :half], next_q[:, :half])
         nc.sync.dma_start(table[:, half:], next_q[:, half:])
 
-        stacked = held.tile([ROWS, SAMPLES], F32, name="stacked")
-        nc.vector.memset(stacked[:], 0.0)
-        for i in range(PIECES):
-            columns = slice(i * PIECE, (i + 1) * PIECE)
-            nc.vector.tensor_copy(stacked[: STEPS + 1, columns], loaded[:, columns])
+        ones = held.tile([ROWS, QUANTILES], F32, name="ones")
+        nc.gpsimd.memset(ones[:], 1.0)
+        warming = psum_held.tile([QUANTILES, QUANTILES], F32, name="warming")
+        for repeat in range(WARMING_MATMULS):
+            nc.tensor.matmul(warming[:], ones[:], ones[:], start=True, stop=True)
 
-        pick_done = held.tile([ROWS, QUANTILES], F32, name="pick_done")
-        nc.gpsimd.memset(pick_done[:], 0.0)
-        nc.gpsimd.memset(pick_done[: STEPS + 1, :], 1.0)
-        nc.gpsimd.memset(pick_done[:STEPS, :], 0.0)
-        discount = held.tile([ROWS, QUANTILES], F32, name="discount")
-        nc.gpsimd.memset(discount[:], 0.0)
-        for t in reversed(range(STEPS)):
-            nc.gpsimd.memset(discount[: t + 1, :], GAMMA**t)
-
+        padded_done = held.tile([ROWS, SAMPLES], F32, name="padded_done")
         coef_all = held.tile([QUANTILES, SAMPLES], F32, name="coef_all")
         for i in range(PIECES):
             columns = slice(i * PIECE, (i + 1) * PIECE)
-            done_all = psum.tile([QUANTILES, PIECE], F32, name=f"done_all{i}")
-            nc.tensor.matmul(done_all[:], pick_done[:], stacked[:, columns], start=True, stop=True)
+            nc.vector.memset(padded_done[:, columns], 0.0)
+            nc.vector.tensor_copy(padded_done[:1, columns], done_row[:, columns])
+            done_all = psum_moving.tile([QUANTILES, PIECE], F32, name="done_all")
+            nc.tensor.matmul(done_all[:], ones[:], padded_done[:, columns], start=True, stop=True)
             nc.scalar.activation(
                 coef_all[:, columns], done_all[:], COPY, bias=GAMMA**STEPS, scale=-(GAMMA**STEPS)
             )
 
-        r_all = [psum.tile([QUANTILES, PIECE], F32, name=f"r_all{i}") for i in range(PIECES)]
+        padded_reward = held.tile([ROWS, SAMPLES], F32, name="padded_reward")
+        nc.gpsimd.memset(padded_reward[:], 0.0)
+        nc.sync.dma_start(padded_reward[: STEPS - 1, :], reward[: STEPS - 1, :])
+        nc.sync.dma_start(padded_reward[STEPS - 1 : STEPS, :], reward[STEPS - 1 :, :])
+
+        discount = held.tile([ROWS, QUANTILES], F32, name="discount")
+        nc.gpsimd.memset(discount[:], GAMMA ** (STEPS - 1))
+        for t in reversed(range(STEPS - 1)):
+            nc.gpsimd.memset(discount[: t + 1, :], GAMMA**t)
+
+        r_all = [psum_held.tile([QUANTILES, PIECE], F32, name=f"r_all{i}") for i in range(PIECES)]
+        r_copy = held.tile([QUANTILES, GPSIMD_PIECES * PIECE], F32, name="r_copy")
         for i in range(PIECES):
             columns = slice(i * PIECE, (i + 1) * PIECE)
-            nc.tensor.matmul(r_all[i][:], discount[:], stacked[:, columns], start=True, stop=True)
+            nc.tensor.matmul(r_all[i][:], discount[:], padded_reward[:, columns], start=True, stop=True)
+            if i < GPSIMD_PIECES:
+                nc.scalar.copy(r_copy[:, columns], r_all[i][:])
 
+        damped = held.tile([QUANTILES, SAMPLES], F32, name="damped")
         for i in range(PIECES):
             columns = slice(i * PIECE, (i + 1) * PIECE)
             entries = slice(i * PIECE // OFFSETS_PER_COLUMN, (i + 1) * PIECE // OFFSETS_PER_COLUMN)
-            damped = moving.tile([QUANTILES, PIECE], F32, name="damped")
             nc.vector.tensor_tensor(
-                damped[:], table[:].indirect(offsets[:, entries]), coef_all[:, columns], ALU.mult
+                damped[:, columns], table[:].indirect(offsets[:, entries]), coef_all[:, columns], ALU.mult
             )
-            target = moving.tile([QUANTILES, PIECE], F32, name="target")
-            nc.vector.tensor_tensor(target[:], damped[:], r_all[i][:], ALU.add)
+
+        target = held.tile([QUANTILES, SAMPLES], F32, name="target")
+        for i in range(PIECES):
+            columns = slice(i * PIECE, (i + 1) * PIECE)
+            if i < GPSIMD_PIECES:
+                nc.gpsimd.tensor_tensor(target[:, columns], damped[:, columns], r_copy[:, columns], ALU.add)
+            else:
+                nc.vector.tensor_tensor(target[:, columns], damped[:, columns], r_all[i][:], ALU.add)
             store_queue = nc.sync if i % 2 == 0 else nc.scalar
-            store_queue.dma_start(out[:, columns], target[:])
+            store_queue.dma_start(out[:, columns], target[:, columns])

@@ -18,7 +18,7 @@ ROWS = 128
 
 WARMING_MATMULS = 3
 
-GPSIMD_PIECES = PIECES // 2
+GPSIMD_PIECE = PIECES - 1
 
 
 def tile_qrdqnnsteptderror_kernel(tc, next_q, reward, done, offs, out):
@@ -66,12 +66,12 @@ def tile_qrdqnnsteptderror_kernel(tc, next_q, reward, done, offs, out):
             nc.gpsimd.memset(discount[: t + 1, :], GAMMA**t)
 
         r_all = [psum_held.tile([QUANTILES, PIECE], F32, name=f"r_all{i}") for i in range(PIECES)]
-        r_copy = held.tile([QUANTILES, GPSIMD_PIECES * PIECE], F32, name="r_copy")
-        for i in range(PIECES):
+        r_copy = held.tile([QUANTILES, PIECE], F32, name="r_copy")
+        for i in [GPSIMD_PIECE] + list(range(GPSIMD_PIECE)):
             columns = slice(i * PIECE, (i + 1) * PIECE)
             nc.tensor.matmul(r_all[i][:], discount[:], padded_reward[:, columns], start=True, stop=True)
-            if i < GPSIMD_PIECES:
-                nc.scalar.copy(r_copy[:, columns], r_all[i][:])
+            if i == GPSIMD_PIECE:
+                nc.scalar.copy(r_copy[:], r_all[i][:])
 
         damped = held.tile([QUANTILES, SAMPLES], F32, name="damped")
         for i in range(PIECES):
@@ -84,8 +84,8 @@ def tile_qrdqnnsteptderror_kernel(tc, next_q, reward, done, offs, out):
         target = held.tile([QUANTILES, SAMPLES], F32, name="target")
         for i in range(PIECES):
             columns = slice(i * PIECE, (i + 1) * PIECE)
-            if i < GPSIMD_PIECES:
-                nc.gpsimd.tensor_tensor(target[:, columns], damped[:, columns], r_copy[:, columns], ALU.add)
+            if i == GPSIMD_PIECE:
+                nc.gpsimd.tensor_tensor(target[:, columns], damped[:, columns], r_copy[:], ALU.add)
             else:
                 nc.vector.tensor_tensor(target[:, columns], damped[:, columns], r_all[i][:], ALU.add)
             store_queue = nc.sync if i % 2 == 0 else nc.scalar

@@ -1,9 +1,9 @@
 import concourse.mybir as mybir
+from concourse.masks import make_identity
 
 F32 = mybir.dt.float32
 U16 = mybir.dt.uint16
 ALU = mybir.AluOpType
-COPY = mybir.ActivationFunctionType.Copy
 
 QUANTILES = 128
 PAIRS = 4096
@@ -14,11 +14,22 @@ GAMMA = 0.99
 PIECE = 512
 PIECES = SAMPLES // PIECE
 OFFSETS_PER_COLUMN = 16
-ROWS = 128
-
-WARMING_MATMULS = 3
+BLOCK = 128
+BLOCKS = SAMPLES // BLOCK
+BLOCKS_PER_PIECE = PIECE // BLOCK
+USED_ROWS = (1 + STEPS) * BLOCKS
 
 GPSIMD_PIECE = PIECES - 1
+
+
+def spread_piece(nc, bank, per_partition, piece, identity):
+    for k in range(BLOCKS_PER_PIECE):
+        block = piece * BLOCKS_PER_PIECE + k
+        nc.tensor.transpose(
+            bank[:, k * BLOCK : (k + 1) * BLOCK],
+            per_partition[:, block : block + 1].to_broadcast([BLOCK, QUANTILES]),
+            identity[:],
+        )
 
 
 def tile_qrdqnnsteptderror_kernel(tc, next_q, reward, done, offs, out):
@@ -28,8 +39,13 @@ def tile_qrdqnnsteptderror_kernel(tc, next_q, reward, done, offs, out):
         tc.psum_pool(name="psum_held", bufs=1) as psum_held,
         tc.psum_pool(name="psum_moving", bufs=3) as psum_moving,
     ):
-        done_row = held.tile([1, SAMPLES], F32, name="done_row")
-        nc.sync.dma_start(done_row[:], done)
+        sample_rows = held.tile([BLOCK, BLOCK], F32, name="sample_rows")
+        reward_as_rows = reward.rearrange("t (b p) -> (t b) p", p=BLOCK)
+        split = (STEPS - 1) * BLOCKS
+        nc.sync.dma_start(sample_rows[:BLOCKS, :], done.rearrange("o (b p) -> (o b) p", p=BLOCK))
+        nc.sync.dma_start(sample_rows[BLOCKS : BLOCKS + split, :], reward_as_rows[:split, :])
+        nc.sync.dma_start(sample_rows[BLOCKS + split : USED_ROWS, :], reward_as_rows[split:, :])
+        nc.vector.memset(sample_rows[USED_ROWS:, :], 0.0)
         offsets = held.tile([QUANTILES, SAMPLES // OFFSETS_PER_COLUMN], U16, name="offsets")
         nc.sync.dma_start(offsets[:], offs)
         table = held.tile([QUANTILES, PAIRS], F32, name="table")
@@ -37,41 +53,35 @@ def tile_qrdqnnsteptderror_kernel(tc, next_q, reward, done, offs, out):
         nc.sync.dma_start(table[:, :half], next_q[:, :half])
         nc.sync.dma_start(table[:, half:], next_q[:, half:])
 
-        ones = held.tile([ROWS, QUANTILES], F32, name="ones")
-        nc.gpsimd.memset(ones[:], 1.0)
-        warming = psum_held.tile([QUANTILES, QUANTILES], F32, name="warming")
-        for repeat in range(WARMING_MATMULS):
-            nc.tensor.matmul(warming[:], ones[:], ones[:], start=True, stop=True)
+        identity = held.tile([BLOCK, BLOCK], F32, name="identity")
+        make_identity(nc, identity[:])
 
-        padded_done = held.tile([ROWS, SAMPLES], F32, name="padded_done")
-        coef_all = held.tile([QUANTILES, SAMPLES], F32, name="coef_all")
-        for i in range(PIECES):
-            columns = slice(i * PIECE, (i + 1) * PIECE)
-            nc.vector.memset(padded_done[:, columns], 0.0)
-            nc.vector.tensor_copy(padded_done[:1, columns], done_row[:, columns])
-            done_all = psum_moving.tile([QUANTILES, PIECE], F32, name="done_all")
-            nc.tensor.matmul(done_all[:], ones[:], padded_done[:, columns], start=True, stop=True)
-            nc.scalar.activation(
-                coef_all[:, columns], done_all[:], COPY, bias=GAMMA**STEPS, scale=-(GAMMA**STEPS)
+        sample_cols = psum_held.tile([BLOCK, BLOCK], F32, name="sample_cols")
+        nc.tensor.transpose(sample_cols[:], sample_rows[:], identity[:])
+
+        coef_col = held.tile([BLOCK, BLOCKS], F32, name="coef_col")
+        nc.vector.tensor_scalar(
+            coef_col[:], sample_cols[:, :BLOCKS], -(GAMMA**STEPS), GAMMA**STEPS, ALU.mult, ALU.add
+        )
+
+        r_col = held.tile([BLOCK, BLOCKS], F32, name="r_col")
+        nc.vector.tensor_copy(r_col[:], sample_cols[:, STEPS * BLOCKS : USED_ROWS])
+        for t in reversed(range(STEPS - 1)):
+            nc.vector.scalar_tensor_tensor(
+                r_col[:], r_col[:], GAMMA, sample_cols[:, (1 + t) * BLOCKS : (2 + t) * BLOCKS], ALU.mult, ALU.add
             )
 
-        padded_reward = held.tile([ROWS, SAMPLES], F32, name="padded_reward")
-        nc.gpsimd.memset(padded_reward[:], 0.0)
-        nc.sync.dma_start(padded_reward[: STEPS - 1, :], reward[: STEPS - 1, :])
-        nc.sync.dma_start(padded_reward[STEPS - 1 : STEPS, :], reward[STEPS - 1 :, :])
-
-        discount = held.tile([ROWS, QUANTILES], F32, name="discount")
-        nc.gpsimd.memset(discount[:], GAMMA ** (STEPS - 1))
-        for t in reversed(range(STEPS - 1)):
-            nc.gpsimd.memset(discount[: t + 1, :], GAMMA**t)
+        coef_all = held.tile([QUANTILES, SAMPLES], F32, name="coef_all")
+        for i in range(PIECES):
+            coef_bank = psum_moving.tile([QUANTILES, PIECE], F32, name="coef_bank")
+            spread_piece(nc, coef_bank, coef_col, i, identity)
+            nc.scalar.copy(coef_all[:, i * PIECE : (i + 1) * PIECE], coef_bank[:])
 
         r_all = [psum_held.tile([QUANTILES, PIECE], F32, name=f"r_all{i}") for i in range(PIECES)]
         r_copy = held.tile([QUANTILES, PIECE], F32, name="r_copy")
-        for i in [GPSIMD_PIECE] + list(range(GPSIMD_PIECE)):
-            columns = slice(i * PIECE, (i + 1) * PIECE)
-            nc.tensor.matmul(r_all[i][:], discount[:], padded_reward[:, columns], start=True, stop=True)
-            if i == GPSIMD_PIECE:
-                nc.scalar.copy(r_copy[:], r_all[i][:])
+        for i in range(PIECES):
+            spread_piece(nc, r_all[i], r_col, i, identity)
+        nc.scalar.copy(r_copy[:], r_all[GPSIMD_PIECE][:])
 
         damped = held.tile([QUANTILES, SAMPLES], F32, name="damped")
         for i in range(PIECES):

@@ -19,16 +19,19 @@ BLOCKS = SAMPLES // BLOCK
 BLOCKS_PER_PIECE = PIECE // BLOCK
 USED_ROWS = (1 + STEPS) * BLOCKS
 
-GPSIMD_PIECE = PIECES - 1
+TENSOR_PIECES = PIECES // 2
 
 
-def spread_piece(nc, bank, per_partition, piece, identity):
+def spread_piece(nc, bank, per_partition, piece, identity, stop):
     for k in range(BLOCKS_PER_PIECE):
         block = piece * BLOCKS_PER_PIECE + k
-        nc.tensor.transpose(
+        nc.tensor.matmul(
             bank[:, k * BLOCK : (k + 1) * BLOCK],
             per_partition[:, block : block + 1].to_broadcast([BLOCK, QUANTILES]),
             identity[:],
+            is_transpose=True,
+            start=(k == 0),
+            stop=(stop and k == BLOCKS_PER_PIECE - 1),
         )
 
 
@@ -74,14 +77,12 @@ def tile_qrdqnnsteptderror_kernel(tc, next_q, reward, done, offs, out):
         coef_all = held.tile([QUANTILES, SAMPLES], F32, name="coef_all")
         for i in range(PIECES):
             coef_bank = psum_moving.tile([QUANTILES, PIECE], F32, name="coef_bank")
-            spread_piece(nc, coef_bank, coef_col, i, identity)
+            spread_piece(nc, coef_bank, coef_col, i, identity, stop=True)
             nc.scalar.copy(coef_all[:, i * PIECE : (i + 1) * PIECE], coef_bank[:])
 
         r_all = [psum_held.tile([QUANTILES, PIECE], F32, name=f"r_all{i}") for i in range(PIECES)]
-        r_copy = held.tile([QUANTILES, PIECE], F32, name="r_copy")
         for i in range(PIECES):
-            spread_piece(nc, r_all[i], r_col, i, identity)
-        nc.scalar.copy(r_copy[:], r_all[GPSIMD_PIECE][:])
+            spread_piece(nc, r_all[i], r_col, i, identity, stop=(i >= TENSOR_PIECES))
 
         damped = held.tile([QUANTILES, SAMPLES], F32, name="damped")
         for i in range(PIECES):
@@ -94,9 +95,10 @@ def tile_qrdqnnsteptderror_kernel(tc, next_q, reward, done, offs, out):
         target = held.tile([QUANTILES, SAMPLES], F32, name="target")
         for i in range(PIECES):
             columns = slice(i * PIECE, (i + 1) * PIECE)
-            if i == GPSIMD_PIECE:
-                nc.gpsimd.tensor_tensor(target[:, columns], damped[:, columns], r_copy[:], ALU.add)
+            if i < TENSOR_PIECES:
+                nc.tensor.matmul(r_all[i][:], identity[:], damped[:, columns], start=False, stop=True)
+                nc.scalar.copy(target[:, columns], r_all[i][:])
+                nc.scalar.dma_start(out[:, columns], target[:, columns])
             else:
                 nc.vector.tensor_tensor(target[:, columns], damped[:, columns], r_all[i][:], ALU.add)
-            store_queue = nc.sync if i % 2 == 0 else nc.scalar
-            store_queue.dma_start(out[:, columns], target[:, columns])
+                nc.sync.dma_start(out[:, columns], target[:, columns])

@@ -45,9 +45,9 @@ def tile_qrdqnnsteptderror_kernel(tc, next_q, reward, done, offs, out):
         sample_rows = held.tile([BLOCK, BLOCK], F32, name="sample_rows")
         reward_as_rows = reward.rearrange("t (b p) -> (t b) p", p=BLOCK)
         split = (STEPS - 1) * BLOCKS
-        nc.sync.dma_start(sample_rows[:BLOCKS, :], done.rearrange("o (b p) -> (o b) p", p=BLOCK))
-        nc.sync.dma_start(sample_rows[BLOCKS : BLOCKS + split, :], reward_as_rows[:split, :])
-        nc.sync.dma_start(sample_rows[BLOCKS + split : USED_ROWS, :], reward_as_rows[split:, :])
+        nc.scalar.dma_start(sample_rows[:BLOCKS, :], done.rearrange("o (b p) -> (o b) p", p=BLOCK))
+        nc.scalar.dma_start(sample_rows[BLOCKS : BLOCKS + split, :], reward_as_rows[:split, :])
+        nc.scalar.dma_start(sample_rows[BLOCKS + split : USED_ROWS, :], reward_as_rows[split:, :])
         nc.vector.memset(sample_rows[USED_ROWS:, :], 0.0)
         offsets = held.tile([QUANTILES, SAMPLES // OFFSETS_PER_COLUMN], U16, name="offsets")
         nc.sync.dma_start(offsets[:], offs)

@@ -21,6 +21,8 @@ USED_ROWS = (1 + STEPS) * BLOCKS
 
 TENSOR_PIECES = PIECES // 2
 
+WARMING_MATMULS = 3
+
 
 def spread_piece(nc, bank, per_partition, piece, identity, stop):
     for k in range(BLOCKS_PER_PIECE):
@@ -60,6 +62,8 @@ def tile_qrdqnnsteptderror_kernel(tc, next_q, reward, done, offs, out):
         make_identity(nc, identity[:])
 
         sample_cols = psum_held.tile([BLOCK, BLOCK], F32, name="sample_cols")
+        for repeat in range(WARMING_MATMULS):
+            nc.tensor.matmul(sample_cols[:], identity[:], identity[:], start=True, stop=True)
         nc.tensor.transpose(sample_cols[:], sample_rows[:], identity[:])
 
         coef_col = held.tile([BLOCK, BLOCKS], F32, name="coef_col")

@@ -16,24 +16,26 @@ PIECES = SAMPLES // PIECE
 OFFSETS_PER_COLUMN = 16
 BLOCK = 128
 BLOCKS = SAMPLES // BLOCK
-BLOCKS_PER_PIECE = PIECE // BLOCK
 USED_ROWS = (1 + STEPS) * BLOCKS
 
 TENSOR_PIECES = PIECES // 2
 
 WARMING_MATMULS = 3
 
+GATHER_CUTS = [0, PIECE // 2] + [i * PIECE for i in range(1, PIECES + 1)]
 
-def spread_piece(nc, bank, per_partition, piece, identity, stop):
-    for k in range(BLOCKS_PER_PIECE):
-        block = piece * BLOCKS_PER_PIECE + k
+
+def spread(nc, bank, per_partition, first, width, identity, stop):
+    blocks = width // BLOCK
+    for k in range(blocks):
+        block = first // BLOCK + k
         nc.tensor.matmul(
             bank[:, k * BLOCK : (k + 1) * BLOCK],
             per_partition[:, block : block + 1].to_broadcast([BLOCK, QUANTILES]),
             identity[:],
             is_transpose=True,
             start=(k == 0),
-            stop=(stop and k == BLOCKS_PER_PIECE - 1),
+            stop=(stop and k == blocks - 1),
         )
 
 
@@ -79,21 +81,20 @@ def tile_qrdqnnsteptderror_kernel(tc, next_q, reward, done, offs, out):
             )
 
         coef_all = held.tile([QUANTILES, SAMPLES], F32, name="coef_all")
-        for i in range(PIECES):
+        for first, end in zip(GATHER_CUTS[:-1], GATHER_CUTS[1:]):
             coef_bank = psum_moving.tile([QUANTILES, PIECE], F32, name="coef_bank")
-            spread_piece(nc, coef_bank, coef_col, i, identity, stop=True)
-            nc.scalar.copy(coef_all[:, i * PIECE : (i + 1) * PIECE], coef_bank[:])
+            spread(nc, coef_bank, coef_col, first, end - first, identity, stop=True)
+            nc.scalar.copy(coef_all[:, first:end], coef_bank[:, : end - first])
 
         r_all = [psum_held.tile([QUANTILES, PIECE], F32, name=f"r_all{i}") for i in range(PIECES)]
         for i in range(PIECES):
-            spread_piece(nc, r_all[i], r_col, i, identity, stop=(i >= TENSOR_PIECES))
+            spread(nc, r_all[i], r_col, i * PIECE, PIECE, identity, stop=(i >= TENSOR_PIECES))
 
         damped = held.tile([QUANTILES, SAMPLES], F32, name="damped")
-        for i in range(PIECES):
-            columns = slice(i * PIECE, (i + 1) * PIECE)
-            entries = slice(i * PIECE // OFFSETS_PER_COLUMN, (i + 1) * PIECE // OFFSETS_PER_COLUMN)
+        for first, end in zip(GATHER_CUTS[:-1], GATHER_CUTS[1:]):
+            entries = slice(first // OFFSETS_PER_COLUMN, end // OFFSETS_PER_COLUMN)
             nc.vector.tensor_tensor(
-                damped[:, columns], table[:].indirect(offsets[:, entries]), coef_all[:, columns], ALU.mult
+                damped[:, first:end], table[:].indirect(offsets[:, entries]), coef_all[:, first:end], ALU.mult
             )
 
         target = held.tile([QUANTILES, SAMPLES], F32, name="target")

@@ -20,8 +20,6 @@ USED_ROWS = (1 + STEPS) * BLOCKS
 
 TENSOR_PIECES = PIECES // 2
 
-WARMING_MATMULS = 3
-
 GATHER_CUTS = [0, PIECE // 2] + [i * PIECE for i in range(1, PIECES + 1)]
 
 
@@ -64,8 +62,6 @@ def tile_qrdqnnsteptderror_kernel(tc, next_q, reward, done, offs, out):
         make_identity(nc, identity[:])
 
         sample_cols = psum_held.tile([BLOCK, BLOCK], F32, name="sample_cols")
-        for repeat in range(WARMING_MATMULS):
-            nc.tensor.matmul(sample_cols[:], identity[:], identity[:], start=True, stop=True)
         nc.tensor.transpose(sample_cols[:], sample_rows[:], identity[:])
 
         coef_col = held.tile([BLOCK, BLOCKS], F32, name="coef_col")

@@ -23,7 +23,10 @@ TENSOR_PIECES = PIECES // 2
 GATHER_CUTS = [0, PIECE // 2] + [i * PIECE for i in range(1, PIECES + 1)]
 
 
-def spread(nc, bank, per_partition, first, width, identity, stop):
+WARMING_MATMULS = 3
+
+
+def spread(nc, bank, per_partition, first, width, identity, stop, as_transpose):
     blocks = width // BLOCK
     for k in range(blocks):
         block = first // BLOCK + k
@@ -31,7 +34,7 @@ def spread(nc, bank, per_partition, first, width, identity, stop):
             bank[:, k * BLOCK : (k + 1) * BLOCK],
             per_partition[:, block : block + 1].to_broadcast([BLOCK, QUANTILES]),
             identity[:],
-            is_transpose=True,
+            is_transpose=as_transpose,
             start=(k == 0),
             stop=(stop and k == blocks - 1),
         )
@@ -47,9 +50,9 @@ def tile_qrdqnnsteptderror_kernel(tc, next_q, reward, done, offs, out):
         sample_rows = held.tile([BLOCK, BLOCK], F32, name="sample_rows")
         reward_as_rows = reward.rearrange("t (b p) -> (t b) p", p=BLOCK)
         split = (STEPS - 1) * BLOCKS
-        nc.scalar.dma_start(sample_rows[:BLOCKS, :], done.rearrange("o (b p) -> (o b) p", p=BLOCK))
-        nc.scalar.dma_start(sample_rows[BLOCKS : BLOCKS + split, :], reward_as_rows[:split, :])
-        nc.scalar.dma_start(sample_rows[BLOCKS + split : USED_ROWS, :], reward_as_rows[split:, :])
+        nc.sync.dma_start(sample_rows[:BLOCKS, :], done.rearrange("o (b p) -> (o b) p", p=BLOCK))
+        nc.sync.dma_start(sample_rows[BLOCKS : BLOCKS + split, :], reward_as_rows[:split, :])
+        nc.sync.dma_start(sample_rows[BLOCKS + split : USED_ROWS, :], reward_as_rows[split:, :])
         nc.vector.memset(sample_rows[USED_ROWS:, :], 0.0)
         offsets = held.tile([QUANTILES, SAMPLES // OFFSETS_PER_COLUMN], U16, name="offsets")
         nc.sync.dma_start(offsets[:], offs)
@@ -58,10 +61,15 @@ def tile_qrdqnnsteptderror_kernel(tc, next_q, reward, done, offs, out):
         nc.sync.dma_start(table[:, :half], next_q[:, :half])
         nc.sync.dma_start(table[:, half:], next_q[:, half:])
 
+        sample_cols = psum_held.tile([BLOCK, BLOCK], F32, name="sample_cols")
         identity = held.tile([BLOCK, BLOCK], F32, name="identity")
         make_identity(nc, identity[:])
 
-        sample_cols = psum_held.tile([BLOCK, BLOCK], F32, name="sample_cols")
+        zeros = held.tile([BLOCK, BLOCK], F32, name="zeros")
+        nc.vector.memset(zeros[:], 0.0)
+        for warming in range(WARMING_MATMULS):
+            nc.tensor.matmul(sample_cols[:], zeros[:], zeros[:], start=True, stop=True)
+
         nc.tensor.transpose(sample_cols[:], sample_rows[:], identity[:])
 
         coef_col = held.tile([BLOCK, BLOCKS], F32, name="coef_col")
@@ -79,12 +87,13 @@ def tile_qrdqnnsteptderror_kernel(tc, next_q, reward, done, offs, out):
         coef_all = held.tile([QUANTILES, SAMPLES], F32, name="coef_all")
         for first, end in zip(GATHER_CUTS[:-1], GATHER_CUTS[1:]):
             coef_bank = psum_moving.tile([QUANTILES, PIECE], F32, name="coef_bank")
-            spread(nc, coef_bank, coef_col, first, end - first, identity, stop=True)
+            spread(nc, coef_bank, coef_col, first, end - first, identity, stop=True, as_transpose=True)
             nc.scalar.copy(coef_all[:, first:end], coef_bank[:, : end - first])
 
         r_all = [psum_held.tile([QUANTILES, PIECE], F32, name=f"r_all{i}") for i in range(PIECES)]
-        for i in range(PIECES):
-            spread(nc, r_all[i], r_col, i * PIECE, PIECE, identity, stop=(i >= TENSOR_PIECES))
+        for i in reversed(range(PIECES)):
+            vectors = i >= TENSOR_PIECES
+            spread(nc, r_all[i], r_col, i * PIECE, PIECE, identity, stop=vectors, as_transpose=vectors)
 
         damped = held.tile([QUANTILES, SAMPLES], F32, name="damped")
         for first, end in zip(GATHER_CUTS[:-1], GATHER_CUTS[1:]):

@@ -11,23 +11,27 @@ SAMPLES = 2048
 STEPS = 5
 GAMMA = 0.99
 
-PIECE = 512
-PIECES = SAMPLES // PIECE
+PART = 256
+PARTS = SAMPLES // PART
+PSUM_RING = 7
 OFFSETS_PER_COLUMN = 16
 BLOCK = 128
 BLOCKS = SAMPLES // BLOCK
 USED_ROWS = (1 + STEPS) * BLOCKS
 
-TENSOR_PIECES = PIECES // 2
-
-GATHER_CUTS = [0, PIECE // 2] + [i * PIECE for i in range(1, PIECES + 1)]
-
+TENSOR_PARTS = PARTS - 2
+VECTOR_COLUMNS = (PARTS - TENSOR_PARTS) * PART
 
 WARMING_MATMULS = 3
+ORDINARY_PARTS = PARTS // 2
 
 
-def spread(nc, bank, per_partition, first, width, identity, stop, as_transpose):
-    blocks = width // BLOCK
+def columns(part):
+    return slice(part * PART, (part + 1) * PART)
+
+
+def spread(nc, bank, per_partition, first, identity, stop, as_transpose):
+    blocks = bank.shape[1] // BLOCK
     for k in range(blocks):
         block = first // BLOCK + k
         nc.tensor.matmul(
@@ -45,7 +49,7 @@ def tile_qrdqnnsteptderror_kernel(tc, next_q, reward, done, offs, out):
     with (
         tc.tile_pool(name="held", bufs=1) as held,
         tc.psum_pool(name="psum_held", bufs=1) as psum_held,
-        tc.psum_pool(name="psum_moving", bufs=3) as psum_moving,
+        tc.psum_pool(name="psum_ring", bufs=PSUM_RING) as psum_ring,
     ):
         sample_rows = held.tile([BLOCK, BLOCK], F32, name="sample_rows")
         reward_as_rows = reward.rearrange("t (b p) -> (t b) p", p=BLOCK)
@@ -85,30 +89,34 @@ def tile_qrdqnnsteptderror_kernel(tc, next_q, reward, done, offs, out):
             )
 
         coef_all = held.tile([QUANTILES, SAMPLES], F32, name="coef_all")
-        for first, end in zip(GATHER_CUTS[:-1], GATHER_CUTS[1:]):
-            coef_bank = psum_moving.tile([QUANTILES, PIECE], F32, name="coef_bank")
-            spread(nc, coef_bank, coef_col, first, end - first, identity, stop=True, as_transpose=True)
-            nc.scalar.copy(coef_all[:, first:end], coef_bank[:, : end - first])
+        for part in range(PARTS):
+            coef_bank = psum_ring.tile([QUANTILES, PART], F32, name="coef_bank", tag="bank")
+            spread(nc, coef_bank, coef_col, part * PART, identity, stop=True, as_transpose=True)
+            nc.scalar.copy(coef_all[:, columns(part)], coef_bank[:])
 
-        r_all = [psum_held.tile([QUANTILES, PIECE], F32, name=f"r_all{i}") for i in range(PIECES)]
-        for i in reversed(range(PIECES)):
-            vectors = i >= TENSOR_PIECES
-            spread(nc, r_all[i], r_col, i * PIECE, PIECE, identity, stop=vectors, as_transpose=vectors)
+        r_vector = psum_ring.tile([QUANTILES, VECTOR_COLUMNS], F32, name="r_vector", tag="bank")
+        spread(nc, r_vector, r_col, TENSOR_PARTS * PART, identity, stop=True, as_transpose=True)
+        r_banks = {}
+        for part in list(range(ORDINARY_PARTS, TENSOR_PARTS)) + list(range(ORDINARY_PARTS)):
+            r_bank = psum_ring.tile([QUANTILES, PART], F32, name="r_bank", tag="bank")
+            spread(nc, r_bank, r_col, part * PART, identity, stop=False, as_transpose=(part >= ORDINARY_PARTS))
+            r_banks[part] = r_bank
 
         damped = held.tile([QUANTILES, SAMPLES], F32, name="damped")
-        for first, end in zip(GATHER_CUTS[:-1], GATHER_CUTS[1:]):
-            entries = slice(first // OFFSETS_PER_COLUMN, end // OFFSETS_PER_COLUMN)
-            nc.vector.tensor_tensor(
-                damped[:, first:end], table[:].indirect(offsets[:, entries]), coef_all[:, first:end], ALU.mult
-            )
-
         target = held.tile([QUANTILES, SAMPLES], F32, name="target")
-        for i in range(PIECES):
-            columns = slice(i * PIECE, (i + 1) * PIECE)
-            if i < TENSOR_PIECES:
-                nc.tensor.matmul(r_all[i][:], identity[:], damped[:, columns], start=False, stop=True)
-                nc.scalar.copy(target[:, columns], r_all[i][:])
-                nc.scalar.dma_start(out[:, columns], target[:, columns])
-            else:
-                nc.vector.tensor_tensor(target[:, columns], damped[:, columns], r_all[i][:], ALU.add)
-                nc.sync.dma_start(out[:, columns], target[:, columns])
+        for part in range(PARTS):
+            here = columns(part)
+            entries = slice(here.start // OFFSETS_PER_COLUMN, here.stop // OFFSETS_PER_COLUMN)
+            nc.vector.tensor_tensor(
+                damped[:, here], table[:].indirect(offsets[:, entries]), coef_all[:, here], ALU.mult
+            )
+            if part < TENSOR_PARTS:
+                nc.tensor.matmul(r_banks[part][:], identity[:], damped[:, here], start=False, stop=True)
+                nc.scalar.copy(target[:, here], r_banks[part][:])
+                nc.scalar.dma_start(out[:, here], target[:, here])
+
+        for part in range(TENSOR_PARTS, PARTS):
+            here = columns(part)
+            within = columns(part - TENSOR_PARTS)
+            nc.vector.tensor_tensor(target[:, here], damped[:, here], r_vector[:, within], ALU.add)
+            nc.sync.dma_start(out[:, here], target[:, here])

@@ -11,6 +11,7 @@ SAMPLES = 2048
 STEPS = 5
 GAMMA = 0.99
 
+BANK = 512
 PART = 256
 PARTS = SAMPLES // PART
 PSUM_RING = 7
@@ -23,7 +24,7 @@ TENSOR_PARTS = PARTS - 2
 VECTOR_COLUMNS = (PARTS - TENSOR_PARTS) * PART
 
 WARMING_MATMULS = 3
-ORDINARY_PARTS = PARTS // 2
+ORDINARY_PARTS = TENSOR_PARTS // 2
 
 
 def columns(part):
@@ -51,6 +52,9 @@ def tile_qrdqnnsteptderror_kernel(tc, next_q, reward, done, offs, out):
         tc.psum_pool(name="psum_held", bufs=1) as psum_held,
         tc.psum_pool(name="psum_ring", bufs=PSUM_RING) as psum_ring,
     ):
+        table = held.tile([QUANTILES, PAIRS], F32, name="table")
+        ahead = PAIRS // 4
+        nc.sync.dma_start(table[:, :ahead], next_q[:, :ahead])
         sample_rows = held.tile([BLOCK, BLOCK], F32, name="sample_rows")
         reward_as_rows = reward.rearrange("t (b p) -> (t b) p", p=BLOCK)
         split = (STEPS - 1) * BLOCKS
@@ -60,14 +64,15 @@ def tile_qrdqnnsteptderror_kernel(tc, next_q, reward, done, offs, out):
         nc.vector.memset(sample_rows[USED_ROWS:, :], 0.0)
         offsets = held.tile([QUANTILES, SAMPLES // OFFSETS_PER_COLUMN], U16, name="offsets")
         nc.sync.dma_start(offsets[:], offs)
-        table = held.tile([QUANTILES, PAIRS], F32, name="table")
-        half = PAIRS // 2
-        nc.sync.dma_start(table[:, :half], next_q[:, :half])
-        nc.sync.dma_start(table[:, half:], next_q[:, half:])
+        nc.sync.dma_start(table[:, ahead:], next_q[:, ahead:])
 
         sample_cols = psum_held.tile([BLOCK, BLOCK], F32, name="sample_cols")
         identity = held.tile([BLOCK, BLOCK], F32, name="identity")
         make_identity(nc, identity[:])
+
+        discount = held.tile([BLOCK, STEPS * BLOCKS], F32, name="discount")
+        for t in range(STEPS):
+            nc.vector.memset(discount[:, t * BLOCKS : (t + 1) * BLOCKS], GAMMA**t)
 
         zeros = held.tile([BLOCK, BLOCK], F32, name="zeros")
         nc.vector.memset(zeros[:], 0.0)
@@ -81,18 +86,22 @@ def tile_qrdqnnsteptderror_kernel(tc, next_q, reward, done, offs, out):
             coef_col[:], sample_cols[:, :BLOCKS], -(GAMMA**STEPS), GAMMA**STEPS, ALU.mult, ALU.add
         )
 
+        discounted = held.tile([BLOCK, STEPS * BLOCKS], F32, name="discounted")
+        nc.vector.tensor_tensor(discounted[:], sample_cols[:, BLOCKS:USED_ROWS], discount[:], ALU.mult)
         r_col = held.tile([BLOCK, BLOCKS], F32, name="r_col")
-        nc.vector.tensor_copy(r_col[:], sample_cols[:, STEPS * BLOCKS : USED_ROWS])
-        for t in reversed(range(STEPS - 1)):
-            nc.vector.scalar_tensor_tensor(
-                r_col[:], r_col[:], GAMMA, sample_cols[:, (1 + t) * BLOCKS : (2 + t) * BLOCKS], ALU.mult, ALU.add
-            )
+        nc.vector.reduce_sum(
+            r_col[:], discounted[:].rearrange("p (t b) -> p b t", t=STEPS), axis=mybir.AxisListType.X
+        )
 
         coef_all = held.tile([QUANTILES, SAMPLES], F32, name="coef_all")
-        for part in range(PARTS):
-            coef_bank = psum_ring.tile([QUANTILES, PART], F32, name="coef_bank", tag="bank")
-            spread(nc, coef_bank, coef_col, part * PART, identity, stop=True, as_transpose=True)
-            nc.scalar.copy(coef_all[:, columns(part)], coef_bank[:])
+        for first in range(0, SAMPLES, BANK):
+            here = slice(first, first + BANK)
+            coef_bank = psum_ring.tile([QUANTILES, BANK], F32, name="coef_bank", tag="bank")
+            spread(nc, coef_bank, coef_col, first, identity, stop=True, as_transpose=True)
+            if first == 0:
+                nc.vector.tensor_copy(coef_all[:, here], coef_bank[:])
+            else:
+                nc.scalar.copy(coef_all[:, here], coef_bank[:])
 
         r_vector = psum_ring.tile([QUANTILES, VECTOR_COLUMNS], F32, name="r_vector", tag="bank")
         spread(nc, r_vector, r_col, TENSOR_PARTS * PART, identity, stop=True, as_transpose=True)

@@ -14,7 +14,8 @@ GAMMA = 0.99
 BANK = 512
 PART = 256
 PARTS = SAMPLES // PART
-PSUM_RING = 7
+COEF_BANKS = 2
+R_BANKS = 5
 OFFSETS_PER_COLUMN = 16
 BLOCK = 128
 BLOCKS = SAMPLES // BLOCK
@@ -23,8 +24,8 @@ USED_ROWS = (1 + STEPS) * BLOCKS
 TENSOR_PARTS = PARTS - 2
 VECTOR_COLUMNS = (PARTS - TENSOR_PARTS) * PART
 
-WARMING_MATMULS = 3
-ORDINARY_PARTS = TENSOR_PARTS // 2
+WARMING_MATMULS = 4
+ORDINARY_PARTS = BANK // PART
 
 
 def columns(part):
@@ -50,7 +51,8 @@ def tile_qrdqnnsteptderror_kernel(tc, next_q, reward, done, offs, out):
     with (
         tc.tile_pool(name="held", bufs=1) as held,
         tc.psum_pool(name="psum_held", bufs=1) as psum_held,
-        tc.psum_pool(name="psum_ring", bufs=PSUM_RING) as psum_ring,
+        tc.psum_pool(name="psum_coef", bufs=COEF_BANKS) as psum_coef,
+        tc.psum_pool(name="psum_r", bufs=R_BANKS) as psum_r,
     ):
         table = held.tile([QUANTILES, PAIRS], F32, name="table")
         ahead = PAIRS // 4
@@ -70,14 +72,14 @@ def tile_qrdqnnsteptderror_kernel(tc, next_q, reward, done, offs, out):
         identity = held.tile([BLOCK, BLOCK], F32, name="identity")
         make_identity(nc, identity[:])
 
-        discount = held.tile([BLOCK, STEPS * BLOCKS], F32, name="discount")
-        for t in range(STEPS):
-            nc.vector.memset(discount[:, t * BLOCKS : (t + 1) * BLOCKS], GAMMA**t)
-
         zeros = held.tile([BLOCK, BLOCK], F32, name="zeros")
         nc.vector.memset(zeros[:], 0.0)
         for warming in range(WARMING_MATMULS):
             nc.tensor.matmul(sample_cols[:], zeros[:], zeros[:], start=True, stop=True)
+
+        discount = held.tile([BLOCK, STEPS * BLOCKS], F32, name="discount")
+        for t in range(STEPS):
+            nc.vector.memset(discount[:, t * BLOCKS : (t + 1) * BLOCKS], GAMMA**t)
 
         nc.tensor.transpose(sample_cols[:], sample_rows[:], identity[:])
 
@@ -96,20 +98,21 @@ def tile_qrdqnnsteptderror_kernel(tc, next_q, reward, done, offs, out):
         coef_all = held.tile([QUANTILES, SAMPLES], F32, name="coef_all")
         for first in range(0, SAMPLES, BANK):
             here = slice(first, first + BANK)
-            coef_bank = psum_ring.tile([QUANTILES, BANK], F32, name="coef_bank", tag="bank")
+            coef_bank = psum_coef.tile([QUANTILES, BANK], F32, name="coef_bank", tag="bank")
             spread(nc, coef_bank, coef_col, first, identity, stop=True, as_transpose=True)
             if first == 0:
                 nc.vector.tensor_copy(coef_all[:, here], coef_bank[:])
             else:
                 nc.scalar.copy(coef_all[:, here], coef_bank[:])
 
-        r_vector = psum_ring.tile([QUANTILES, VECTOR_COLUMNS], F32, name="r_vector", tag="bank")
-        spread(nc, r_vector, r_col, TENSOR_PARTS * PART, identity, stop=True, as_transpose=True)
-        r_banks = {}
-        for part in list(range(ORDINARY_PARTS, TENSOR_PARTS)) + list(range(ORDINARY_PARTS)):
-            r_bank = psum_ring.tile([QUANTILES, PART], F32, name="r_bank", tag="bank")
+        r_banks = []
+        for part in range(TENSOR_PARTS):
+            pool = psum_r if part < R_BANKS else psum_coef
+            r_bank = pool.tile([QUANTILES, PART], F32, name="r_bank", tag="bank")
             spread(nc, r_bank, r_col, part * PART, identity, stop=False, as_transpose=(part >= ORDINARY_PARTS))
-            r_banks[part] = r_bank
+            r_banks.append(r_bank)
+        r_vector = psum_coef.tile([QUANTILES, VECTOR_COLUMNS], F32, name="r_vector", tag="bank")
+        spread(nc, r_vector, r_col, TENSOR_PARTS * PART, identity, stop=True, as_transpose=True)
 
         damped = held.tile([QUANTILES, SAMPLES], F32, name="damped")
         target = held.tile([QUANTILES, SAMPLES], F32, name="target")

@@ -25,7 +25,7 @@ TENSOR_PARTS = PARTS - 2
 VECTOR_COLUMNS = (PARTS - TENSOR_PARTS) * PART
 
 WARMING_MATMULS = 4
-ORDINARY_PARTS = BANK // PART
+ORDINARY_PARTS = TENSOR_PARTS // 2
 
 
 def columns(part):
@@ -55,7 +55,7 @@ def tile_qrdqnnsteptderror_kernel(tc, next_q, reward, done, offs, out):
         tc.psum_pool(name="psum_r", bufs=R_BANKS) as psum_r,
     ):
         table = held.tile([QUANTILES, PAIRS], F32, name="table")
-        ahead = PAIRS // 4
+        ahead = PAIRS // 8
         nc.sync.dma_start(table[:, :ahead], next_q[:, :ahead])
         sample_rows = held.tile([BLOCK, BLOCK], F32, name="sample_rows")
         reward_as_rows = reward.rearrange("t (b p) -> (t b) p", p=BLOCK)

@@ -24,7 +24,6 @@ USED_ROWS = (1 + STEPS) * BLOCKS
 TENSOR_PARTS = PARTS - 2
 VECTOR_COLUMNS = (PARTS - TENSOR_PARTS) * PART
 
-WARMING_MATMULS = 4
 ORDINARY_PARTS = TENSOR_PARTS // 2
 
 
@@ -71,11 +70,6 @@ def tile_qrdqnnsteptderror_kernel(tc, next_q, reward, done, offs, out):
         sample_cols = psum_held.tile([BLOCK, BLOCK], F32, name="sample_cols")
         identity = held.tile([BLOCK, BLOCK], F32, name="identity")
         make_identity(nc, identity[:])
-
-        zeros = held.tile([BLOCK, BLOCK], F32, name="zeros")
-        nc.vector.memset(zeros[:], 0.0)
-        for warming in range(WARMING_MATMULS):
-            nc.tensor.matmul(sample_cols[:], zeros[:], zeros[:], start=True, stop=True)
 
         discount = held.tile([BLOCK, STEPS * BLOCKS], F32, name="discount")
         for t in range(STEPS):

import concourse.mybir as mybir
from concourse.masks import make_identity

F32 = mybir.dt.float32
U16 = mybir.dt.uint16
ALU = mybir.AluOpType

QUANTILES = 128
PAIRS = 4096
SAMPLES = 2048
STEPS = 5
GAMMA = 0.99

BANK = 512
PART = 256
PARTS = SAMPLES // PART
COEF_BANKS = 2
R_BANKS = 5
OFFSETS_PER_COLUMN = 16
BLOCK = 128
BLOCKS = SAMPLES // BLOCK
USED_ROWS = (1 + STEPS) * BLOCKS

TENSOR_PARTS = PARTS - 2
VECTOR_COLUMNS = (PARTS - TENSOR_PARTS) * PART

ORDINARY_PARTS = TENSOR_PARTS // 2


def columns(part):
    return slice(part * PART, (part + 1) * PART)


def spread(nc, bank, per_partition, first, identity, stop, as_transpose):
    blocks = bank.shape[1] // BLOCK
    for k in range(blocks):
        block = first // BLOCK + k
        nc.tensor.matmul(
            bank[:, k * BLOCK : (k + 1) * BLOCK],
            per_partition[:, block : block + 1].to_broadcast([BLOCK, QUANTILES]),
            identity[:],
            is_transpose=as_transpose,
            start=(k == 0),
            stop=(stop and k == blocks - 1),
        )


def tile_qrdqnnsteptderror_kernel(tc, next_q, reward, done, offs, out):
    nc = tc.nc
    with (
        tc.tile_pool(name="held", bufs=1) as held,
        tc.psum_pool(name="psum_held", bufs=1) as psum_held,
        tc.psum_pool(name="psum_coef", bufs=COEF_BANKS) as psum_coef,
        tc.psum_pool(name="psum_r", bufs=R_BANKS) as psum_r,
    ):
        table = held.tile([QUANTILES, PAIRS], F32, name="table")
        ahead = PAIRS // 8
        nc.sync.dma_start(table[:, :ahead], next_q[:, :ahead])
        sample_rows = held.tile([BLOCK, BLOCK], F32, name="sample_rows")
        reward_as_rows = reward.rearrange("t (b p) -> (t b) p", p=BLOCK)
        split = (STEPS - 1) * BLOCKS
        nc.sync.dma_start(sample_rows[:BLOCKS, :], done.rearrange("o (b p) -> (o b) p", p=BLOCK))
        nc.sync.dma_start(sample_rows[BLOCKS : BLOCKS + split, :], reward_as_rows[:split, :])
        nc.sync.dma_start(sample_rows[BLOCKS + split : USED_ROWS, :], reward_as_rows[split:, :])
        nc.vector.memset(sample_rows[USED_ROWS:, :], 0.0)
        offsets = held.tile([QUANTILES, SAMPLES // OFFSETS_PER_COLUMN], U16, name="offsets")
        nc.sync.dma_start(offsets[:], offs)
        nc.sync.dma_start(table[:, ahead:], next_q[:, ahead:])

        sample_cols = psum_held.tile([BLOCK, BLOCK], F32, name="sample_cols")
        identity = held.tile([BLOCK, BLOCK], F32, name="identity")
        make_identity(nc, identity[:])

        discount = held.tile([BLOCK, STEPS * BLOCKS], F32, name="discount")
        for t in range(STEPS):
            nc.vector.memset(discount[:, t * BLOCKS : (t + 1) * BLOCKS], GAMMA**t)

        nc.tensor.transpose(sample_cols[:], sample_rows[:], identity[:])

        coef_col = held.tile([BLOCK, BLOCKS], F32, name="coef_col")
        nc.vector.tensor_scalar(
            coef_col[:], sample_cols[:, :BLOCKS], -(GAMMA**STEPS), GAMMA**STEPS, ALU.mult, ALU.add
        )

        discounted = held.tile([BLOCK, STEPS * BLOCKS], F32, name="discounted")
        nc.vector.tensor_tensor(discounted[:], sample_cols[:, BLOCKS:USED_ROWS], discount[:], ALU.mult)
        r_col = held.tile([BLOCK, BLOCKS], F32, name="r_col")
        nc.vector.reduce_sum(
            r_col[:], discounted[:].rearrange("p (t b) -> p b t", t=STEPS), axis=mybir.AxisListType.X
        )

        coef_all = held.tile([QUANTILES, SAMPLES], F32, name="coef_all")
        for first in range(0, SAMPLES, BANK):
            here = slice(first, first + BANK)
            coef_bank = psum_coef.tile([QUANTILES, BANK], F32, name="coef_bank", tag="bank")
            spread(nc, coef_bank, coef_col, first, identity, stop=True, as_transpose=True)
            if first == 0:
                nc.vector.tensor_copy(coef_all[:, here], coef_bank[:])
            else:
                nc.scalar.copy(coef_all[:, here], coef_bank[:])

        r_banks = []
        for part in range(TENSOR_PARTS):
            pool = psum_r if part < R_BANKS else psum_coef
            r_bank = pool.tile([QUANTILES, PART], F32, name="r_bank", tag="bank")
            spread(nc, r_bank, r_col, part * PART, identity, stop=False, as_transpose=(part >= ORDINARY_PARTS))
            r_banks.append(r_bank)
        r_vector = psum_coef.tile([QUANTILES, VECTOR_COLUMNS], F32, name="r_vector", tag="bank")
        spread(nc, r_vector, r_col, TENSOR_PARTS * PART, identity, stop=True, as_transpose=True)

        damped = held.tile([QUANTILES, SAMPLES], F32, name="damped")
        target = held.tile([QUANTILES, SAMPLES], F32, name="target")
        for part in range(PARTS):
            here = columns(part)
            entries = slice(here.start // OFFSETS_PER_COLUMN, here.stop // OFFSETS_PER_COLUMN)
            nc.vector.tensor_tensor(
                damped[:, here], table[:].indirect(offsets[:, entries]), coef_all[:, here], ALU.mult
            )
            if part < TENSOR_PARTS:
                nc.tensor.matmul(r_banks[part][:], identity[:], damped[:, here], start=False, stop=True)
                nc.scalar.copy(target[:, here], r_banks[part][:])
                nc.scalar.dma_start(out[:, here], target[:, here])

        for part in range(TENSOR_PARTS, PARTS):
            here = columns(part)
            within = columns(part - TENSOR_PARTS)
            nc.vector.tensor_tensor(target[:, here], damped[:, here], r_vector[:, within], ALU.add)
            nc.sync.dma_start(out[:, here], target[:, here])
